import numpy as np
import ml_dtypes


def mxq(x, axis, fmt="e4m3"):
    dtype, down = {"e4m3": (ml_dtypes.float8_e4m3fn, 7), "e5m2": (ml_dtypes.float8_e5m2, 14)}[fmt]
    v = np.moveaxis(np.asarray(x, np.float32).astype(ml_dtypes.bfloat16).astype(np.float64), axis, -1)
    blocks = v.reshape(v.shape[:-1] + (-1, 32))
    amax = np.abs(blocks).max(-1, keepdims=True)
    byte = np.maximum(np.where(amax > 0, np.frexp(amax)[1] - 1 + 127, 0) - down, 1)
    scale = np.exp2(byte - 127.0)
    codes = (blocks / scale).astype(np.float32).astype(dtype).astype(np.float64)
    return np.moveaxis((codes * scale).reshape(v.shape), -1, axis)


WIDE = False


def mx_kscale(k):
    if not WIDE:
        return np.ones(k)
    levels = np.array([10, -10, 5, -5, 0])
    if k % 512:
        return np.exp2(np.random.permutation(np.resize(levels, k // 32))).repeat(32)
    a = np.empty((k // 512, 16))
    for p in range(k // 512):
        a[p, :8] = np.random.permutation(np.resize(levels, 8))
        for g in range(8):
            far = levels[np.abs(levels - a[p, g]) >= 10]
            a[p, g + 8] = far[np.random.randint(len(far))]
    return np.exp2(a.ravel()).repeat(32)


BF16 = ml_dtypes.bfloat16


def bf(x):
    return np.asarray(x, np.float32).astype(BF16)


def f64(x):
    return np.asarray(x).astype(np.float64)


B, T, D, H = 1, 512, 2048, 16
HD = D // H
SCALE = HD ** (-0.5)


def rotate_half(u):
    u1, u2 = np.split(u, 2, axis=-1)
    return np.concatenate([-u2, u1], axis=-1)


def apply_rope(u, sin, cos):
    return u * cos[None, :, None, :] + rotate_half(u) * sin[None, :, None, :]


def setup_inputs():
    s = mx_kscale(D)
    return {"x": bf(np.random.standard_normal((B, T, D)) * s),
            "sin": bf(np.random.standard_normal((T, HD))),
            "cos": bf(np.random.standard_normal((T, HD))),
            "W_qkv": bf(np.random.standard_normal((D, D + 2 * HD)) * 2.0 / np.sqrt(D) / s[:, None])}


def reference(x, sin, cos, W_qkv):
    sin, cos = f64(sin), f64(cos)
    qkv = mxq(f64(x), 2, "e4m3") @ mxq(f64(W_qkv), 0, "e4m3")
    q, k, v = np.split(qkv, [D, D + HD], axis=-1)
    q = q.reshape(B, T, H, HD) * SCALE
    q_rot = np.ascontiguousarray(apply_rope(q, sin, cos).transpose(0, 2, 1, 3))
    k_rot = apply_rope(k[:, :, None, :], sin, cos)[:, :, 0, :]
    return q_rot, k_rot, v

@@ -1,0 +1,283 @@
+from contextlib import ExitStack
+
+import concourse.mybir as mybir
+from concourse.masks import make_identity
+
+F32 = mybir.dt.float32
+BF16 = mybir.dt.bfloat16
+U32 = mybir.dt.uint32
+U8 = mybir.dt.uint8
+FP8X4 = mybir.dt.float8_e4m3fn_x4
+MULT = mybir.AluOpType.mult
+ADD = mybir.AluOpType.add
+
+P = 128
+PACK = 4
+K_PASS = P * PACK
+TOKENS = 512
+D_MODEL = 2048
+HEAD_DIM = 128
+HALF = HEAD_DIM // 2
+Q_HEADS = 16
+N_COLS = (Q_HEADS + 2) * HEAD_DIM
+PASSES = D_MODEL // K_PASS
+TOKEN_BLOCKS = TOKENS // P
+GROUP_COLS = 512
+Q_SCALE = HEAD_DIM**-0.5
+RUN = 4
+X_AHEAD = 2
+PSUM_BANKS = 8
+VECTOR_EIGHTHS_FIRST = 3
+VECTOR_EIGHTHS = 1
+
+FLOPS = 2 * TOKENS * D_MODEL * N_COLS
+
+
+def tile_multiqueryattention_pa_kernel(tc, x, sin, cos, W_qkv, out_0, out_1, out_2):
+    nc = tc.nc
+    groups = [(first, min(GROUP_COLS, N_COLS - first)) for first in range(0, N_COLS, GROUP_COLS)]
+
+    x_blocks = x.rearrange("b (m r) k -> (b m) r k", r=TOKEN_BLOCKS)
+    cos_blocks = cos.rearrange("(m r) d -> m r d", r=TOKEN_BLOCKS)
+    sin_blocks = sin.rearrange("(m r) d -> m r d", r=TOKEN_BLOCKS)
+    q_view = out_0.rearrange("b h (m r) d -> m (b h) (r d)", r=TOKEN_BLOCKS)
+    k_view = out_1.rearrange("b (m r) d -> m b (r d)", r=TOKEN_BLOCKS)
+    v_view = out_2.rearrange("b (m r) d -> m b (r d)", r=TOKEN_BLOCKS)
+
+    with ExitStack() as ctx:
+        const = ctx.enter_context(tc.tile_pool(name="const", bufs=1))
+        x_pool = ctx.enter_context(tc.tile_pool(name="x_pool", bufs=PASSES))
+        x_stage = ctx.enter_context(tc.tile_pool(name="x_stage", bufs=2))
+        raw_pool = ctx.enter_context(tc.tile_pool(name="raw_pool", bufs=len(groups) * PASSES))
+        grouped_pool = ctx.enter_context(tc.tile_pool(name="grouped_pool", bufs=4))
+        codes_pool = ctx.enter_context(tc.tile_pool(name="codes_pool", bufs=3))
+        product_pool = ctx.enter_context(tc.tile_pool(name="product_pool", bufs=4))
+        out_pool = ctx.enter_context(tc.tile_pool(name="out_pool", bufs=3))
+        psum_even = ctx.enter_context(tc.psum_pool(name="psum_even", bufs=PSUM_BANKS // 2))
+        psum_odd = ctx.enter_context(tc.psum_pool(name="psum_odd", bufs=PSUM_BANKS // 2))
+        ctx.enter_context(tc.manual_schedule())
+
+        def load_x_chunk(c):
+            x_rows = x_pool.tile([P, TOKEN_BLOCKS * K_PASS], BF16)
+            for b in range(TOKEN_BLOCKS // 2):
+                nc.sync.dma_start(
+                    out=x_rows[:, 2 * b * K_PASS : (2 * b + 2) * K_PASS].rearrange(
+                        "p (r k) -> p r k", r=2
+                    ),
+                    in_=x_blocks[:, 2 * b : 2 * b + 2, c * K_PASS : (c + 1) * K_PASS],
+                )
+            return x_rows
+
+        def load_w_chunk(g, c):
+            first, width = groups[g]
+            w_raw = raw_pool.tile([P, PACK, width], BF16)
+            w_rows = W_qkv[K_PASS * c : K_PASS * (c + 1), first : first + width].rearrange(
+                "(p t) w -> p t w", t=PACK
+            )
+            for u in range(2):
+                nc.sync.dma_start(
+                    out=w_raw[:, 2 * u : 2 * u + 2, :], in_=w_rows[:, 2 * u : 2 * u + 2, :]
+                )
+            return w_raw
+
+        cos_raw = const.tile([P, TOKEN_BLOCKS, HEAD_DIM], BF16)
+        sin_raw = const.tile([P, TOKEN_BLOCKS, HEAD_DIM], BF16)
+
+        w_raw_of = {}
+        x_rows_of = []
+        for c in range(PASSES):
+            w_raw_of[(0, c)] = load_w_chunk(0, c)
+            x_rows_of.append(load_x_chunk(c))
+        nc.sync.dma_start(out=cos_raw[:], in_=cos_blocks)
+        nc.sync.dma_start(out=sin_raw[:], in_=sin_blocks)
+        for g in range(1, len(groups)):
+            for c in range(PASSES):
+                w_raw_of[(g, c)] = load_w_chunk(g, c)
+
+        identity = const.tile([P, P], F32)
+        make_identity(nc, identity[:])
+
+        def make_tables(factor, cos_table, sin_table):
+            nc.gpsimd.tensor_scalar(
+                out=cos_table[:], in0=cos_raw[:], scalar1=factor, scalar2=0.0, op0=MULT, op1=ADD
+            )
+            nc.gpsimd.tensor_scalar(
+                out=sin_table[:, :, 0:HALF], in0=sin_raw[:, :, 0:HALF],
+                scalar1=-factor, scalar2=0.0, op0=MULT, op1=ADD,
+            )
+            nc.gpsimd.tensor_scalar(
+                out=sin_table[:, :, HALF:HEAD_DIM], in0=sin_raw[:, :, HALF:HEAD_DIM],
+                scalar1=factor, scalar2=0.0, op0=MULT, op1=ADD,
+            )
+
+        cos_q = const.tile([P, TOKEN_BLOCKS, HEAD_DIM], F32)
+        sin_q = const.tile([P, TOKEN_BLOCKS, HEAD_DIM], F32)
+        cos_k = const.tile([P, TOKEN_BLOCKS, HEAD_DIM], F32)
+        sin_k = const.tile([P, TOKEN_BLOCKS, HEAD_DIM], F32)
+        make_tables(Q_SCALE, cos_q, sin_q)
+        make_tables(1.0, cos_k, sin_k)
+
+        x_codes = const.tile([P, PASSES, TOKENS], U32, align_bytes=64)
+        x_scales = const.tile([P, PASSES, TOKENS], U8, align_bytes=64)
+
+        def transpose_x_chunk(c):
+            x_words = x_rows_of[c][:].bitcast(F32)
+            x_banks = []
+            for b in range(TOKEN_BLOCKS // 2):
+                bank = psum_odd.tile([P, GROUP_COLS], F32, tag="bank")
+                for u in range(2):
+                    for rr in range(2):
+                        word = 2 * P * (2 * b + rr)
+                        nc.tensor.transpose(
+                            bank[:, (2 * u + rr) * P : (2 * u + rr + 1) * P],
+                            x_words[:, word + u : word + 2 * P : 2],
+                            identity[:],
+                        )
+                x_banks.append(bank)
+            return x_banks
+
+        def collect_x_chunk(x_banks):
+            x_grouped = x_stage.tile([P, TOKENS * PACK], BF16, align_bytes=64)
+            grouped_words = x_grouped[:].bitcast(F32).rearrange("p (n u) -> p n u", u=2)
+            nc.vector.tensor_copy(
+                out=grouped_words[:, 0 : 2 * P, :],
+                in_=x_banks[0][:].rearrange("p (u n) -> p n u", u=2),
+            )
+            nc.scalar.copy(
+                out=grouped_words[:, 2 * P : 4 * P, :],
+                in_=x_banks[1][:].rearrange("p (u n) -> p n u", u=2),
+            )
+            return x_grouped
+
+        def quantise_x_chunk(c, x_grouped):
+            nc.vector.quantize_mx(
+                out=x_codes[:, c, :].bitcast(FP8X4), scales=x_scales[:, c, :], in_=x_grouped[:]
+            )
+
+        def regroup_w_chunk(g, c, vector_eighths):
+            width = groups[g][1]
+            split = width - width * vector_eighths // 8
+            w_grouped = grouped_pool.tile([P, width, PACK], BF16, align_bytes=64)
+            w_raw = w_raw_of[(g, c)]
+            nc.scalar.copy(
+                out=w_grouped[:, 0:split, :].rearrange("p (n i) t -> p n t i", i=RUN),
+                in_=w_raw[:, :, 0:split].rearrange("p t (n i) -> p n t i", i=RUN),
+            )
+            nc.vector.tensor_copy(
+                out=w_grouped[:, split:width, :].rearrange("p (n i) t -> p n t i", i=RUN),
+                in_=w_raw[:, :, split:width].rearrange("p t (n i) -> p n t i", i=RUN),
+            )
+            return w_grouped
+
+        def quantise_w_chunk(g, c, w_grouped, w_codes, w_scales):
+            width = groups[g][1]
+            nc.vector.quantize_mx(
+                out=w_codes[:, c, 0:width].bitcast(FP8X4),
+                scales=w_scales[:, c, 0:width],
+                in_=w_grouped[:].rearrange("p n t -> p (n t)"),
+            )
+
+        def open_group(g):
+            w_codes = codes_pool.tile([P, PASSES, GROUP_COLS], U32, align_bytes=64)
+            w_scales = codes_pool.tile([P, PASSES, GROUP_COLS], U8, align_bytes=64)
+            psum_half = psum_even if g % 2 == 0 else psum_odd
+            banks = [
+                psum_half.tile([P, GROUP_COLS], F32, tag="bank", name="acc")
+                for r in range(TOKEN_BLOCKS)
+            ]
+            return w_codes, w_scales, banks
+
+        def multiply_chunk(g, c, w_codes, w_scales, banks):
+            width = groups[g][1]
+            for r in range(TOKEN_BLOCKS):
+                nc.tensor.matmul_mx(
+                    out=banks[r][:, 0:width],
+                    lhsT=x_codes[:, c, r * P : (r + 1) * P].bitcast(FP8X4),
+                    lhsT_scale=x_scales[:, c, r * P : (r + 1) * P],
+                    rhs=w_codes[:, c, 0:width].bitcast(FP8X4),
+                    rhs_scale=w_scales[:, c, 0:width],
+                    start=(c == 0),
+                    stop=(c == PASSES - 1),
+                )
+
+        def rope(heads, u, cos_table, sin_table, rotated):
+            direct = product_pool.tile([P, heads, HEAD_DIM], F32)
+            crossed = product_pool.tile([P, heads, HEAD_DIM], F32)
+            nc.vector.tensor_tensor(
+                out=direct[:], in0=u,
+                in1=cos_table.unsqueeze(1).to_broadcast([P, heads, HEAD_DIM]), op=MULT,
+            )
+            for half in range(2):
+                here = slice(half * HALF, (half + 1) * HALF)
+                other = slice((1 - half) * HALF, (2 - half) * HALF)
+                nc.vector.tensor_tensor(
+                    out=crossed[:, :, here], in0=u[:, :, other],
+                    in1=sin_table[:, here].unsqueeze(1).to_broadcast([P, heads, HALF]), op=MULT,
+                )
+            nc.gpsimd.tensor_tensor(out=rotated, in0=direct[:], in1=crossed[:], op=ADD)
+
+        def finish_bank(g, r, bank, rotated, v_rows):
+            first, width = groups[g]
+            is_q = first < Q_HEADS * HEAD_DIM
+            heads = rotated.shape[1]
+            rope(
+                heads,
+                bank[:, 0 : heads * HEAD_DIM].rearrange("p (h d) -> p h d", d=HEAD_DIM),
+                (cos_q if is_q else cos_k)[:, r, :],
+                (sin_q if is_q else sin_k)[:, r, :],
+                rotated[:, :, r, :],
+            )
+            if not is_q:
+                nc.vector.tensor_copy(out=v_rows[:, 0, r, :], in_=bank[:, HEAD_DIM : 2 * HEAD_DIM])
+            if r == TOKEN_BLOCKS - 1:
+                if is_q:
+                    head = first // HEAD_DIM
+                    nc.sync.dma_start(
+                        out=q_view[:, head : head + heads, :],
+                        in_=rotated[:].rearrange("p h r d -> p h (r d)"),
+                    )
+                else:
+                    nc.sync.dma_start(out=v_view, in_=v_rows[:].rearrange("p h r d -> p h (r d)"))
+                    nc.sync.dma_start(out=k_view, in_=rotated[:].rearrange("p h r d -> p h (r d)"))
+
+        def open_outputs(g):
+            first, width = groups[g]
+            is_q = first < Q_HEADS * HEAD_DIM
+            heads = width // HEAD_DIM if is_q else 1
+            rotated = out_pool.tile([P, heads, TOKEN_BLOCKS, HEAD_DIM], F32, tag="rotated")
+            v_rows = None
+            if not is_q:
+                v_rows = out_pool.tile([P, 1, TOKEN_BLOCKS, HEAD_DIM], F32, tag="v_rows")
+            return rotated, v_rows
+
+        assert PASSES == TOKEN_BLOCKS
+        steps = len(groups) * PASSES
+        x_banks_of = [transpose_x_chunk(c) for c in range(X_AHEAD)]
+        w_grouped_next = regroup_w_chunk(0, 0, VECTOR_EIGHTHS_FIRST)
+        for n in range(steps):
+            g, c = divmod(n, PASSES)
+            w_grouped = w_grouped_next
+            if g == 0:
+                x_grouped = collect_x_chunk(x_banks_of[c])
+            if c == 0:
+                if g > 0:
+                    done_banks = banks
+                    rotated, v_rows = open_outputs(g - 1)
+                w_codes, w_scales, banks = open_group(g)
+            quantise_w_chunk(g, c, w_grouped, w_codes, w_scales)
+            if g == 0:
+                quantise_x_chunk(c, x_grouped)
+            multiply_chunk(g, c, w_codes, w_scales, banks)
+            if n + 1 < steps:
+                w_grouped_next = regroup_w_chunk(
+                    (n + 1) // PASSES,
+                    (n + 1) % PASSES,
+                    VECTOR_EIGHTHS_FIRST if g == 0 else VECTOR_EIGHTHS,
+                )
+            if g == 0 and c + X_AHEAD < PASSES:
+                x_banks_of.append(transpose_x_chunk(c + X_AHEAD))
+            if g > 0:
+                finish_bank(g - 1, c, done_banks[c], rotated, v_rows)
+        rotated, v_rows = open_outputs(len(groups) - 1)
+        for r in range(TOKEN_BLOCKS):
+            finish_bank(len(groups) - 1, r, banks[r], rotated, v_rows)

@@ -22,12 +22,14 @@ Q_HEADS = 16
 N_COLS = (Q_HEADS + 2) * HEAD_DIM
 PASSES = D_MODEL // K_PASS
 TOKEN_BLOCKS = TOKENS // P
+X_PAIRS = TOKEN_BLOCKS // 2
 GROUP_COLS = 512
+GROUP_HEADS = GROUP_COLS // HEAD_DIM
+Q_GROUPS = Q_HEADS // GROUP_HEADS
+KV_COLS = 2 * HEAD_DIM
 Q_SCALE = HEAD_DIM**-0.5
 RUN = 4
-X_AHEAD = 2
-PSUM_BANKS = 8
-VECTOR_EIGHTHS_FIRST = 3
+VECTOR_EIGHTHS_FIRST = 2
 VECTOR_EIGHTHS = 1
 
 FLOPS = 2 * TOKENS * D_MODEL * N_COLS
@@ -35,43 +37,37 @@ FLOPS = 2 * TOKENS * D_MODEL * N_COLS
 
 def tile_multiqueryattention_pa_kernel(tc, x, sin, cos, W_qkv, out_0, out_1, out_2):
     nc = tc.nc
-    groups = [(first, min(GROUP_COLS, N_COLS - first)) for first in range(0, N_COLS, GROUP_COLS)]
+    widths = [GROUP_COLS] * Q_GROUPS + [KV_COLS]
 
     x_blocks = x.rearrange("b (m r) k -> (b m) r k", r=TOKEN_BLOCKS)
     cos_blocks = cos.rearrange("(m r) d -> m r d", r=TOKEN_BLOCKS)
     sin_blocks = sin.rearrange("(m r) d -> m r d", r=TOKEN_BLOCKS)
     q_view = out_0.rearrange("b h (m r) d -> m (b h) (r d)", r=TOKEN_BLOCKS)
-    k_view = out_1.rearrange("b (m r) d -> m b (r d)", r=TOKEN_BLOCKS)
-    v_view = out_2.rearrange("b (m r) d -> m b (r d)", r=TOKEN_BLOCKS)
+    k_view = out_1.rearrange("b (m r) d -> (b m) (r d)", r=TOKEN_BLOCKS)
+    v_view = out_2.rearrange("b (m r) d -> (b m) (r d)", r=TOKEN_BLOCKS)
 
     with ExitStack() as ctx:
         const = ctx.enter_context(tc.tile_pool(name="const", bufs=1))
-        x_pool = ctx.enter_context(tc.tile_pool(name="x_pool", bufs=PASSES))
-        x_stage = ctx.enter_context(tc.tile_pool(name="x_stage", bufs=2))
-        raw_pool = ctx.enter_context(tc.tile_pool(name="raw_pool", bufs=len(groups) * PASSES))
+        x_pool = ctx.enter_context(tc.tile_pool(name="x_pool", bufs=TOKEN_BLOCKS))
+        x_stage = ctx.enter_context(tc.tile_pool(name="x_stage", bufs=TOKEN_BLOCKS))
+        raw_pool = ctx.enter_context(tc.tile_pool(name="raw_pool", bufs=len(widths) * PASSES))
         grouped_pool = ctx.enter_context(tc.tile_pool(name="grouped_pool", bufs=4))
         codes_pool = ctx.enter_context(tc.tile_pool(name="codes_pool", bufs=3))
         product_pool = ctx.enter_context(tc.tile_pool(name="product_pool", bufs=4))
         out_pool = ctx.enter_context(tc.tile_pool(name="out_pool", bufs=3))
-        psum_even = ctx.enter_context(tc.psum_pool(name="psum_even", bufs=PSUM_BANKS // 2))
-        psum_odd = ctx.enter_context(tc.psum_pool(name="psum_odd", bufs=PSUM_BANKS // 2))
+        psum_acc = ctx.enter_context(tc.psum_pool(name="psum_acc", bufs=TOKEN_BLOCKS))
+        psum_x = ctx.enter_context(tc.psum_pool(name="psum_x", bufs=4))
         ctx.enter_context(tc.manual_schedule())
 
-        def load_x_chunk(c):
-            x_rows = x_pool.tile([P, TOKEN_BLOCKS * K_PASS], BF16)
-            for b in range(TOKEN_BLOCKS // 2):
-                nc.sync.dma_start(
-                    out=x_rows[:, 2 * b * K_PASS : (2 * b + 2) * K_PASS].rearrange(
-                        "p (r k) -> p r k", r=2
-                    ),
-                    in_=x_blocks[:, 2 * b : 2 * b + 2, c * K_PASS : (c + 1) * K_PASS],
-                )
+        def load_x_block(r):
+            x_rows = x_pool.tile([P, D_MODEL], BF16)
+            nc.sync.dma_start(out=x_rows[:], in_=x_blocks[:, r, :])
             return x_rows
 
         def load_w_chunk(g, c):
-            first, width = groups[g]
-            w_raw = raw_pool.tile([P, PACK, width], BF16)
-            w_rows = W_qkv[K_PASS * c : K_PASS * (c + 1), first : first + width].rearrange(
+            first = g * GROUP_COLS
+            w_raw = raw_pool.tile([P, PACK, widths[g]], BF16)
+            w_rows = W_qkv[K_PASS * c : K_PASS * (c + 1), first : first + widths[g]].rearrange(
                 "(p t) w -> p t w", t=PACK
             )
             for u in range(2):
@@ -83,79 +79,83 @@ def tile_multiqueryattention_pa_kernel(tc, x, sin, cos, W_qkv, out_0, out_1, out
         cos_raw = const.tile([P, TOKEN_BLOCKS, HEAD_DIM], BF16)
         sin_raw = const.tile([P, TOKEN_BLOCKS, HEAD_DIM], BF16)
 
-        w_raw_of = {}
         x_rows_of = []
+        w_raw_of = {}
         for c in range(PASSES):
             w_raw_of[(0, c)] = load_w_chunk(0, c)
-            x_rows_of.append(load_x_chunk(c))
-        nc.sync.dma_start(out=cos_raw[:], in_=cos_blocks)
-        nc.sync.dma_start(out=sin_raw[:], in_=sin_blocks)
-        for g in range(1, len(groups)):
+            if c < X_PAIRS:
+                x_rows_of.append(load_x_block(2 * c))
+                x_rows_of.append(load_x_block(2 * c + 1))
+            if c == X_PAIRS - 1:
+                nc.sync.dma_start(out=cos_raw[:], in_=cos_blocks)
+                nc.sync.dma_start(out=sin_raw[:], in_=sin_blocks)
+        for g in range(1, len(widths)):
             for c in range(PASSES):
                 w_raw_of[(g, c)] = load_w_chunk(g, c)
+
+        table_in = const.tile([P, 1], F32)
+        table_out = const.tile([P, 1], F32)
+        nc.gpsimd.memset(table_in[:], 0.0)
+        nc.scalar.copy(out=table_out[:], in_=table_in[:])
 
         identity = const.tile([P, P], F32)
         make_identity(nc, identity[:])
 
-        def make_tables(factor, cos_table, sin_table):
-            nc.gpsimd.tensor_scalar(
-                out=cos_table[:], in0=cos_raw[:], scalar1=factor, scalar2=0.0, op0=MULT, op1=ADD
-            )
-            nc.gpsimd.tensor_scalar(
-                out=sin_table[:, :, 0:HALF], in0=sin_raw[:, :, 0:HALF],
-                scalar1=-factor, scalar2=0.0, op0=MULT, op1=ADD,
-            )
-            nc.gpsimd.tensor_scalar(
-                out=sin_table[:, :, HALF:HEAD_DIM], in0=sin_raw[:, :, HALF:HEAD_DIM],
-                scalar1=factor, scalar2=0.0, op0=MULT, op1=ADD,
-            )
+        def make_tables(factor):
+            tables = const.tile([P, 2, TOKEN_BLOCKS, HEAD_DIM], F32, name="tables_%d" % (factor == 1.0))
+            for out, in_, signed in (
+                (tables[:, 0], cos_raw[:], factor),
+                (tables[:, 1, :, 0:HALF], sin_raw[:, :, HALF:HEAD_DIM], factor),
+                (tables[:, 1, :, HALF:HEAD_DIM], sin_raw[:, :, 0:HALF], -factor),
+            ):
+                nc.gpsimd.tensor_scalar(
+                    out=out, in0=in_, scalar1=signed, scalar2=0.0, op0=MULT, op1=ADD
+                )
+            return tables
 
-        cos_q = const.tile([P, TOKEN_BLOCKS, HEAD_DIM], F32)
-        sin_q = const.tile([P, TOKEN_BLOCKS, HEAD_DIM], F32)
-        cos_k = const.tile([P, TOKEN_BLOCKS, HEAD_DIM], F32)
-        sin_k = const.tile([P, TOKEN_BLOCKS, HEAD_DIM], F32)
-        make_tables(Q_SCALE, cos_q, sin_q)
-        make_tables(1.0, cos_k, sin_k)
+        tables_q = make_tables(Q_SCALE)
+        tables_k = make_tables(1.0)
 
-        x_codes = const.tile([P, PASSES, TOKENS], U32, align_bytes=64)
-        x_scales = const.tile([P, PASSES, TOKENS], U8, align_bytes=64)
+        x_codes = const.tile([P, TOKEN_BLOCKS, PASSES, P], U32, align_bytes=64)
+        x_scales = const.tile([P, TOKEN_BLOCKS, PASSES, P], U8, align_bytes=64)
 
-        def transpose_x_chunk(c):
-            x_words = x_rows_of[c][:].bitcast(F32)
+        def transpose_x_block(r):
+            x_words = x_rows_of[r][:].bitcast(F32)
             x_banks = []
-            for b in range(TOKEN_BLOCKS // 2):
-                bank = psum_odd.tile([P, GROUP_COLS], F32, tag="bank")
-                for u in range(2):
-                    for rr in range(2):
-                        word = 2 * P * (2 * b + rr)
+            for j in range(PASSES // 2):
+                bank = psum_x.tile([P, GROUP_COLS], F32, tag="x_bank")
+                for cc in range(2):
+                    for u in range(2):
+                        word = 2 * P * (2 * j + cc)
                         nc.tensor.transpose(
-                            bank[:, (2 * u + rr) * P : (2 * u + rr + 1) * P],
+                            bank[:, (2 * cc + u) * P : (2 * cc + u + 1) * P],
                             x_words[:, word + u : word + 2 * P : 2],
                             identity[:],
                         )
                 x_banks.append(bank)
             return x_banks
 
-        def collect_x_chunk(x_banks):
-            x_grouped = x_stage.tile([P, TOKENS * PACK], BF16, align_bytes=64)
-            grouped_words = x_grouped[:].bitcast(F32).rearrange("p (n u) -> p n u", u=2)
-            nc.vector.tensor_copy(
-                out=grouped_words[:, 0 : 2 * P, :],
-                in_=x_banks[0][:].rearrange("p (u n) -> p n u", u=2),
-            )
+        def collect_x_block(x_banks):
+            x_grouped = x_stage.tile([P, PASSES, P, PACK], BF16, align_bytes=64)
+            words = x_grouped[:].rearrange("p c n t -> p (c n t)").bitcast(F32)
+            words = words.rearrange("p (c n u) -> p c n u", c=PASSES, u=2)
             nc.scalar.copy(
-                out=grouped_words[:, 2 * P : 4 * P, :],
-                in_=x_banks[1][:].rearrange("p (u n) -> p n u", u=2),
+                out=words[:, 0:2], in_=x_banks[0][:].rearrange("p (c u n) -> p c n u", c=2, u=2)
+            )
+            nc.vector.tensor_copy(
+                out=words[:, 2:4], in_=x_banks[1][:].rearrange("p (c u n) -> p c n u", c=2, u=2)
             )
             return x_grouped
 
-        def quantise_x_chunk(c, x_grouped):
+        def quantise_x_block(r, x_grouped):
             nc.vector.quantize_mx(
-                out=x_codes[:, c, :].bitcast(FP8X4), scales=x_scales[:, c, :], in_=x_grouped[:]
+                out=x_codes[:, r].rearrange("p c m -> p (c m)").bitcast(FP8X4),
+                scales=x_scales[:, r].rearrange("p c m -> p (c m)"),
+                in_=x_grouped[:].rearrange("p c n t -> p (c n t)"),
             )
 
         def regroup_w_chunk(g, c, vector_eighths):
-            width = groups[g][1]
+            width = widths[g]
             split = width - width * vector_eighths // 8
             w_grouped = grouped_pool.tile([P, width, PACK], BF16, align_bytes=64)
             w_raw = w_raw_of[(g, c)]
@@ -170,114 +170,147 @@ def tile_multiqueryattention_pa_kernel(tc, x, sin, cos, W_qkv, out_0, out_1, out
             return w_grouped
 
         def quantise_w_chunk(g, c, w_grouped, w_codes, w_scales):
-            width = groups[g][1]
             nc.vector.quantize_mx(
-                out=w_codes[:, c, 0:width].bitcast(FP8X4),
-                scales=w_scales[:, c, 0:width],
+                out=w_codes[:, c, 0 : widths[g]].bitcast(FP8X4),
+                scales=w_scales[:, c, 0 : widths[g]],
                 in_=w_grouped[:].rearrange("p n t -> p (n t)"),
             )
 
-        def open_group(g):
+        def open_codes():
             w_codes = codes_pool.tile([P, PASSES, GROUP_COLS], U32, align_bytes=64)
             w_scales = codes_pool.tile([P, PASSES, GROUP_COLS], U8, align_bytes=64)
-            psum_half = psum_even if g % 2 == 0 else psum_odd
-            banks = [
-                psum_half.tile([P, GROUP_COLS], F32, tag="bank", name="acc")
-                for r in range(TOKEN_BLOCKS)
-            ]
-            return w_codes, w_scales, banks
+            return w_codes, w_scales
 
-        def multiply_chunk(g, c, w_codes, w_scales, banks):
-            width = groups[g][1]
-            for r in range(TOKEN_BLOCKS):
-                nc.tensor.matmul_mx(
-                    out=banks[r][:, 0:width],
-                    lhsT=x_codes[:, c, r * P : (r + 1) * P].bitcast(FP8X4),
-                    lhsT_scale=x_scales[:, c, r * P : (r + 1) * P],
-                    rhs=w_codes[:, c, 0:width].bitcast(FP8X4),
-                    rhs_scale=w_scales[:, c, 0:width],
-                    start=(c == 0),
-                    stop=(c == PASSES - 1),
-                )
+        def multiply(out, r, c, w_codes, w_scales):
+            width = out.shape[1]
+            nc.tensor.matmul_mx(
+                out=out,
+                lhsT=x_codes[:, r, c, :].bitcast(FP8X4),
+                lhsT_scale=x_scales[:, r, c, :],
+                rhs=w_codes[:, c, 0:width].bitcast(FP8X4),
+                rhs_scale=w_scales[:, c, 0:width],
+                start=(c == 0),
+                stop=(c == PASSES - 1),
+            )
 
-        def rope(heads, u, cos_table, sin_table, rotated):
-            direct = product_pool.tile([P, heads, HEAD_DIM], F32)
-            crossed = product_pool.tile([P, heads, HEAD_DIM], F32)
+        def open_bank():
+            return psum_acc.tile([P, GROUP_COLS], F32, tag="bank", name="acc")
+
+        def multiply_bank(r, w_codes, w_scales):
+            bank = open_bank()
+            for c in range(PASSES):
+                multiply(bank[:], r, c, w_codes, w_scales)
+            return bank
+
+        def swap_halves(u):
+            return u.rearrange("p h (s d) -> p h s d", s=2)[:, :, ::-1, :]
+
+        def rope_q_bank(r, bank, rotated):
+            products = product_pool.tile([P, 2, GROUP_HEADS, HEAD_DIM], F32)
+            shape = [P, 2, GROUP_HEADS, HEAD_DIM]
+            heads = bank[:].rearrange("p (h d) -> p h d", d=HEAD_DIM)
             nc.vector.tensor_tensor(
-                out=direct[:], in0=u,
-                in1=cos_table.unsqueeze(1).to_broadcast([P, heads, HEAD_DIM]), op=MULT,
+                out=products[:],
+                in0=heads.unsqueeze(1).to_broadcast(shape),
+                in1=tables_q[:, :, r, :].unsqueeze(2).to_broadcast(shape),
+                op=MULT,
             )
-            for half in range(2):
-                here = slice(half * HALF, (half + 1) * HALF)
-                other = slice((1 - half) * HALF, (2 - half) * HALF)
-                nc.vector.tensor_tensor(
-                    out=crossed[:, :, here], in0=u[:, :, other],
-                    in1=sin_table[:, here].unsqueeze(1).to_broadcast([P, heads, HALF]), op=MULT,
-                )
-            nc.gpsimd.tensor_tensor(out=rotated, in0=direct[:], in1=crossed[:], op=ADD)
-
-        def finish_bank(g, r, bank, rotated, v_rows):
-            first, width = groups[g]
-            is_q = first < Q_HEADS * HEAD_DIM
-            heads = rotated.shape[1]
-            rope(
-                heads,
-                bank[:, 0 : heads * HEAD_DIM].rearrange("p (h d) -> p h d", d=HEAD_DIM),
-                (cos_q if is_q else cos_k)[:, r, :],
-                (sin_q if is_q else sin_k)[:, r, :],
-                rotated[:, :, r, :],
+            nc.gpsimd.tensor_tensor(
+                out=rotated[:, :, r, :].rearrange("p h (s d) -> p h s d", s=2),
+                in0=products[:, 0].rearrange("p h (s d) -> p h s d", s=2),
+                in1=swap_halves(products[:, 1]),
+                op=ADD,
             )
-            if not is_q:
-                nc.vector.tensor_copy(out=v_rows[:, 0, r, :], in_=bank[:, HEAD_DIM : 2 * HEAD_DIM])
-            if r == TOKEN_BLOCKS - 1:
-                if is_q:
-                    head = first // HEAD_DIM
-                    nc.sync.dma_start(
-                        out=q_view[:, head : head + heads, :],
-                        in_=rotated[:].rearrange("p h r d -> p h (r d)"),
-                    )
-                else:
-                    nc.sync.dma_start(out=v_view, in_=v_rows[:].rearrange("p h r d -> p h (r d)"))
-                    nc.sync.dma_start(out=k_view, in_=rotated[:].rearrange("p h r d -> p h (r d)"))
-
-        def open_outputs(g):
-            first, width = groups[g]
-            is_q = first < Q_HEADS * HEAD_DIM
-            heads = width // HEAD_DIM if is_q else 1
-            rotated = out_pool.tile([P, heads, TOKEN_BLOCKS, HEAD_DIM], F32, tag="rotated")
-            v_rows = None
-            if not is_q:
-                v_rows = out_pool.tile([P, 1, TOKEN_BLOCKS, HEAD_DIM], F32, tag="v_rows")
-            return rotated, v_rows
 
         assert PASSES == TOKEN_BLOCKS
-        steps = len(groups) * PASSES
-        x_banks_of = [transpose_x_chunk(c) for c in range(X_AHEAD)]
-        w_grouped_next = regroup_w_chunk(0, 0, VECTOR_EIGHTHS_FIRST)
-        for n in range(steps):
+        banks_of = {}
+        codes = open_codes()
+        x_banks_of = [transpose_x_block(r) for r in range(2)]
+
+        def collect_and_transpose_ahead(r):
+            x_grouped = collect_x_block(x_banks_of[r])
+            if r + 2 < TOKEN_BLOCKS:
+                x_banks_of.append(transpose_x_block(r + 2))
+            return x_grouped
+
+        for i in range(X_PAIRS):
+            w_grouped = regroup_w_chunk(0, i, VECTOR_EIGHTHS_FIRST)
+            x_even = collect_and_transpose_ahead(2 * i)
+            quantise_w_chunk(0, i, w_grouped, *codes)
+            x_odd = collect_and_transpose_ahead(2 * i + 1)
+            quantise_x_block(2 * i, x_even)
+            quantise_x_block(2 * i + 1, x_odd)
+            for r in range(2 * i):
+                multiply(banks_of[(0, r)][:], r, i, *codes)
+            for r in range(2 * i, 2 * i + 2):
+                banks_of[(0, r)] = open_bank()
+                for c in range(i + 1):
+                    multiply(banks_of[(0, r)][:], r, c, *codes)
+        for c in range(X_PAIRS, PASSES):
+            w_grouped = regroup_w_chunk(0, c, VECTOR_EIGHTHS_FIRST)
+            quantise_w_chunk(0, c, w_grouped, *codes)
+            for r in range(TOKEN_BLOCKS):
+                multiply(banks_of[(0, r)][:], r, c, *codes)
+
+        w_grouped_next = regroup_w_chunk(1, 0, VECTOR_EIGHTHS)
+        steps = len(widths) * PASSES
+        for n in range(PASSES, steps):
             g, c = divmod(n, PASSES)
             w_grouped = w_grouped_next
-            if g == 0:
-                x_grouped = collect_x_chunk(x_banks_of[c])
             if c == 0:
-                if g > 0:
-                    done_banks = banks
-                    rotated, v_rows = open_outputs(g - 1)
-                w_codes, w_scales, banks = open_group(g)
-            quantise_w_chunk(g, c, w_grouped, w_codes, w_scales)
-            if g == 0:
-                quantise_x_chunk(c, x_grouped)
-            multiply_chunk(g, c, w_codes, w_scales, banks)
+                done_codes = codes
+                rotated = out_pool.tile(
+                    [P, GROUP_HEADS, TOKEN_BLOCKS, HEAD_DIM], F32, tag="rotated"
+                )
+                codes = open_codes()
+            if g > 1 and c + 1 < TOKEN_BLOCKS:
+                banks_of[(g - 1, c + 1)] = multiply_bank(c + 1, *done_codes)
+            if g == 1:
+                rope_q_bank(c, banks_of[(g - 1, c)], rotated)
+            quantise_w_chunk(g, c, w_grouped, *codes)
+            if c == PASSES - 1 and g < Q_GROUPS:
+                banks_of[(g, 0)] = multiply_bank(0, *codes)
             if n + 1 < steps:
                 w_grouped_next = regroup_w_chunk(
-                    (n + 1) // PASSES,
-                    (n + 1) % PASSES,
-                    VECTOR_EIGHTHS_FIRST if g == 0 else VECTOR_EIGHTHS,
+                    (n + 1) // PASSES, (n + 1) % PASSES, VECTOR_EIGHTHS
                 )
-            if g == 0 and c + X_AHEAD < PASSES:
-                x_banks_of.append(transpose_x_chunk(c + X_AHEAD))
-            if g > 0:
-                finish_bank(g - 1, c, done_banks[c], rotated, v_rows)
-        rotated, v_rows = open_outputs(len(groups) - 1)
-        for r in range(TOKEN_BLOCKS):
-            finish_bank(len(groups) - 1, r, banks[r], rotated, v_rows)
+            if g > 1:
+                rope_q_bank(c, banks_of[(g - 1, c)], rotated)
+            if c == TOKEN_BLOCKS - 1:
+                head = (g - 1) * GROUP_HEADS
+                nc.sync.dma_start(
+                    out=q_view[:, head : head + GROUP_HEADS, :],
+                    in_=rotated[:].rearrange("p h r d -> p h (r d)"),
+                )
+
+        k_rows = out_pool.tile([P, TOKEN_BLOCKS, HEAD_DIM], F32, tag="k_rows")
+        v_rows = out_pool.tile([P, TOKEN_BLOCKS, HEAD_DIM], F32, tag="v_rows")
+        kv_banks = []
+        for pair in range(2):
+            bank = psum_acc.tile([P, 2, KV_COLS], F32, tag="bank", name="acc")
+            for rr in range(2):
+                for c in range(PASSES):
+                    multiply(bank[:, rr, :], 2 * pair + rr, c, *codes)
+            kv_banks.append(bank)
+        products_of = []
+        for pair in range(2):
+            blocks = slice(2 * pair, 2 * pair + 2)
+            products = product_pool.tile([P, 2, 2, HEAD_DIM], F32)
+            nc.vector.tensor_tensor(
+                out=products[:],
+                in0=kv_banks[pair][:, :, 0:HEAD_DIM].unsqueeze(1).to_broadcast([P, 2, 2, HEAD_DIM]),
+                in1=tables_k[:, :, blocks, :],
+                op=MULT,
+            )
+            products_of.append(products)
+            nc.scalar.copy(out=v_rows[:, blocks, :], in_=kv_banks[pair][:, :, HEAD_DIM:KV_COLS])
+        for pair in range(2):
+            blocks = slice(2 * pair, 2 * pair + 2)
+            nc.vector.tensor_tensor(
+                out=k_rows[:, blocks, :].rearrange("p h (s d) -> p h s d", s=2),
+                in0=products_of[pair][:, 0].rearrange("p h (s d) -> p h s d", s=2),
+                in1=swap_halves(products_of[pair][:, 1]),
+                op=ADD,
+            )
+        nc.sync.dma_start(out=v_view, in_=v_rows[:].rearrange("p r d -> p (r d)"))
+        nc.sync.dma_start(out=k_view, in_=k_rows[:].rearrange("p r d -> p (r d)"))

@@ -29,8 +29,9 @@ Q_GROUPS = Q_HEADS // GROUP_HEADS
 KV_COLS = 2 * HEAD_DIM
 Q_SCALE = HEAD_DIM**-0.5
 RUN = 4
-VECTOR_EIGHTHS_FIRST = 2
-VECTOR_EIGHTHS = 1
+VECTOR_EIGHTHS_FIRST = 4
+VECTOR_EIGHTHS_LATER = 4
+VECTOR_HELPS_UNTIL = 2
 
 FLOPS = 2 * TOKENS * D_MODEL * N_COLS
 
@@ -42,7 +43,7 @@ def tile_multiqueryattention_pa_kernel(tc, x, sin, cos, W_qkv, out_0, out_1, out
     x_blocks = x.rearrange("b (m r) k -> (b m) r k", r=TOKEN_BLOCKS)
     cos_blocks = cos.rearrange("(m r) d -> m r d", r=TOKEN_BLOCKS)
     sin_blocks = sin.rearrange("(m r) d -> m r d", r=TOKEN_BLOCKS)
-    q_view = out_0.rearrange("b h (m r) d -> m (b h) (r d)", r=TOKEN_BLOCKS)
+    q_view = out_0.rearrange("b h (m r) d -> m (b h) r d", r=TOKEN_BLOCKS)
     k_view = out_1.rearrange("b (m r) d -> (b m) (r d)", r=TOKEN_BLOCKS)
     v_view = out_2.rearrange("b (m r) d -> (b m) (r d)", r=TOKEN_BLOCKS)
 
@@ -163,10 +164,11 @@ def tile_multiqueryattention_pa_kernel(tc, x, sin, cos, W_qkv, out_0, out_1, out
                 out=w_grouped[:, 0:split, :].rearrange("p (n i) t -> p n t i", i=RUN),
                 in_=w_raw[:, :, 0:split].rearrange("p t (n i) -> p n t i", i=RUN),
             )
-            nc.vector.tensor_copy(
-                out=w_grouped[:, split:width, :].rearrange("p (n i) t -> p n t i", i=RUN),
-                in_=w_raw[:, :, split:width].rearrange("p t (n i) -> p n t i", i=RUN),
-            )
+            if split < width:
+                nc.vector.tensor_copy(
+                    out=w_grouped[:, split:width, :].rearrange("p (n i) t -> p n t i", i=RUN),
+                    in_=w_raw[:, :, split:width].rearrange("p t (n i) -> p n t i", i=RUN),
+                )
             return w_grouped
 
         def quantise_w_chunk(g, c, w_grouped, w_codes, w_scales):
@@ -233,26 +235,33 @@ def tile_multiqueryattention_pa_kernel(tc, x, sin, cos, W_qkv, out_0, out_1, out
                 x_banks_of.append(transpose_x_block(r + 2))
             return x_grouped
 
-        for i in range(X_PAIRS):
-            w_grouped = regroup_w_chunk(0, i, VECTOR_EIGHTHS_FIRST)
-            x_even = collect_and_transpose_ahead(2 * i)
-            quantise_w_chunk(0, i, w_grouped, *codes)
-            x_odd = collect_and_transpose_ahead(2 * i + 1)
-            quantise_x_block(2 * i, x_even)
-            quantise_x_block(2 * i + 1, x_odd)
-            for r in range(2 * i):
-                multiply(banks_of[(0, r)][:], r, i, *codes)
-            for r in range(2 * i, 2 * i + 2):
-                banks_of[(0, r)] = open_bank()
-                for c in range(i + 1):
+        def multiply_first_group(blocks, chunks):
+            for c in chunks:
+                for r in blocks:
+                    if c == 0:
+                        banks_of[(0, r)] = open_bank()
                     multiply(banks_of[(0, r)][:], r, c, *codes)
-        for c in range(X_PAIRS, PASSES):
+
+        w_grouped = regroup_w_chunk(0, 0, VECTOR_EIGHTHS_FIRST)
+        quantise_w_chunk(0, 0, w_grouped, *codes)
+        x_grouped_0 = collect_and_transpose_ahead(0)
+        w_grouped = regroup_w_chunk(0, 1, VECTOR_EIGHTHS_FIRST)
+        x_grouped_1 = collect_and_transpose_ahead(1)
+        quantise_x_block(0, x_grouped_0)
+        quantise_w_chunk(0, 1, w_grouped, *codes)
+        quantise_x_block(1, x_grouped_1)
+        multiply_first_group((0, 1), (0, 1))
+        x_grouped_2 = collect_and_transpose_ahead(2)
+        x_grouped_3 = collect_and_transpose_ahead(3)
+        quantise_x_block(2, x_grouped_2)
+        quantise_x_block(3, x_grouped_3)
+        multiply_first_group((2, 3), (0, 1))
+        for c in range(2, PASSES):
             w_grouped = regroup_w_chunk(0, c, VECTOR_EIGHTHS_FIRST)
             quantise_w_chunk(0, c, w_grouped, *codes)
-            for r in range(TOKEN_BLOCKS):
-                multiply(banks_of[(0, r)][:], r, c, *codes)
+            multiply_first_group(range(TOKEN_BLOCKS), (c,))
 
-        w_grouped_next = regroup_w_chunk(1, 0, VECTOR_EIGHTHS)
+        w_grouped_next = regroup_w_chunk(1, 0, VECTOR_EIGHTHS_LATER)
         steps = len(widths) * PASSES
         for n in range(PASSES, steps):
             g, c = divmod(n, PASSES)
@@ -271,16 +280,19 @@ def tile_multiqueryattention_pa_kernel(tc, x, sin, cos, W_qkv, out_0, out_1, out
             if c == PASSES - 1 and g < Q_GROUPS:
                 banks_of[(g, 0)] = multiply_bank(0, *codes)
             if n + 1 < steps:
+                g_next, c_next = divmod(n + 1, PASSES)
+                helps = c_next == 0 and g_next <= VECTOR_HELPS_UNTIL
                 w_grouped_next = regroup_w_chunk(
-                    (n + 1) // PASSES, (n + 1) % PASSES, VECTOR_EIGHTHS
+                    g_next, c_next, VECTOR_EIGHTHS_LATER if helps else 0
                 )
             if g > 1:
                 rope_q_bank(c, banks_of[(g - 1, c)], rotated)
-            if c == TOKEN_BLOCKS - 1:
-                head = (g - 1) * GROUP_HEADS
+            stored = TOKEN_BLOCKS if g < Q_GROUPS else TOKEN_BLOCKS // 2
+            if (c + 1) % stored == 0:
+                heads = slice((g - 1) * GROUP_HEADS, g * GROUP_HEADS)
+                blocks = slice(c + 1 - stored, c + 1)
                 nc.sync.dma_start(
-                    out=q_view[:, head : head + GROUP_HEADS, :],
-                    in_=rotated[:].rearrange("p h r d -> p h (r d)"),
+                    out=q_view[:, heads, blocks, :], in_=rotated[:, :, blocks, :]
                 )
 
         k_rows = out_pool.tile([P, TOKEN_BLOCKS, HEAD_DIM], F32, tag="k_rows")

@@ -30,8 +30,9 @@ KV_COLS = 2 * HEAD_DIM
 Q_SCALE = HEAD_DIM**-0.5
 RUN = 4
 VECTOR_EIGHTHS_FIRST = 4
-VECTOR_EIGHTHS_LATER = 4
-VECTOR_HELPS_UNTIL = 2
+TENSOR_AHEAD = 2
+
+WARM_UP = 4
 
 FLOPS = 2 * TOKENS * D_MODEL * N_COLS
 
@@ -80,13 +81,13 @@ def tile_multiqueryattention_pa_kernel(tc, x, sin, cos, W_qkv, out_0, out_1, out
         cos_raw = const.tile([P, TOKEN_BLOCKS, HEAD_DIM], BF16)
         sin_raw = const.tile([P, TOKEN_BLOCKS, HEAD_DIM], BF16)
 
-        x_rows_of = []
+        x_rows_of = [load_x_block(0)]
         w_raw_of = {}
         for c in range(PASSES):
             w_raw_of[(0, c)] = load_w_chunk(0, c)
             if c < X_PAIRS:
-                x_rows_of.append(load_x_block(2 * c))
-                x_rows_of.append(load_x_block(2 * c + 1))
+                for r in range(2 * c + 1, min(2 * c + 3, TOKEN_BLOCKS)):
+                    x_rows_of.append(load_x_block(r))
             if c == X_PAIRS - 1:
                 nc.sync.dma_start(out=cos_raw[:], in_=cos_blocks)
                 nc.sync.dma_start(out=sin_raw[:], in_=sin_blocks)
@@ -101,6 +102,8 @@ def tile_multiqueryattention_pa_kernel(tc, x, sin, cos, W_qkv, out_0, out_1, out
 
         identity = const.tile([P, P], F32)
         make_identity(nc, identity[:])
+        identity_bf16 = const.tile([P, P], BF16)
+        make_identity(nc, identity_bf16[:])
 
         def make_tables(factor):
             tables = const.tile([P, 2, TOKEN_BLOCKS, HEAD_DIM], F32, name="tables_%d" % (factor == 1.0))
@@ -117,6 +120,17 @@ def tile_multiqueryattention_pa_kernel(tc, x, sin, cos, W_qkv, out_0, out_1, out
         tables_q = make_tables(Q_SCALE)
         tables_k = make_tables(1.0)
 
+        warm_weights = const.tile([P, P], BF16)
+        warm_moving = const.tile([P, GROUP_COLS], BF16)
+        nc.vector.memset(warm_weights[:], 0.0)
+        nc.vector.memset(warm_moving[:], 0.0)
+
+        def keep_tensor_busy(bank, count):
+            for i in range(count):
+                nc.tensor.matmul(
+                    bank[:], lhsT=warm_weights[:], rhs=warm_moving[:], start=True, stop=True
+                )
+
         x_codes = const.tile([P, TOKEN_BLOCKS, PASSES, P], U32, align_bytes=64)
         x_scales = const.tile([P, TOKEN_BLOCKS, PASSES, P], U8, align_bytes=64)
 
@@ -125,6 +139,7 @@ def tile_multiqueryattention_pa_kernel(tc, x, sin, cos, W_qkv, out_0, out_1, out
             x_banks = []
             for j in range(PASSES // 2):
                 bank = psum_x.tile([P, GROUP_COLS], F32, tag="x_bank")
+                keep_tensor_busy(bank, WARM_UP if r == 0 and j == 0 else 1)
                 for cc in range(2):
                     for u in range(2):
                         word = 2 * P * (2 * j + cc)
@@ -169,6 +184,30 @@ def tile_multiqueryattention_pa_kernel(tc, x, sin, cos, W_qkv, out_0, out_1, out
                     out=w_grouped[:, split:width, :].rearrange("p (n i) t -> p n t i", i=RUN),
                     in_=w_raw[:, :, split:width].rearrange("p t (n i) -> p n t i", i=RUN),
                 )
+            return w_grouped
+
+        def interleave_on_tensor(g, c):
+            bank = psum_x.tile([P, GROUP_COLS], F32, tag="x_bank", name="w_bank")
+            words = bank[:].bitcast(BF16)[:, 0 : P * PACK]
+            nc.tensor.matmul(
+                words.rearrange("p (n t) -> p n t", t=PACK),
+                lhsT=identity_bf16[:],
+                rhs=w_raw_of[(g, c)][:, :, widths[g] - P : widths[g]].rearrange("p t n -> p n t"),
+                start=True,
+                stop=True,
+            )
+            return words
+
+        def collect_w_chunk(g, c, interleaved):
+            split = widths[g] - P
+            w_grouped = grouped_pool.tile([P, widths[g], PACK], BF16, align_bytes=64, name="w_grouped")
+            nc.scalar.copy(
+                out=w_grouped[:, 0:split, :].rearrange("p (n i) t -> p n t i", i=RUN),
+                in_=w_raw_of[(g, c)][:, :, 0:split].rearrange("p t (n i) -> p n t i", i=RUN),
+            )
+            nc.scalar.copy(
+                out=w_grouped[:, split:, :].rearrange("p n t -> p (n t)"), in_=interleaved
+            )
             return w_grouped
 
         def quantise_w_chunk(g, c, w_grouped, w_codes, w_scales):
@@ -242,26 +281,28 @@ def tile_multiqueryattention_pa_kernel(tc, x, sin, cos, W_qkv, out_0, out_1, out
                         banks_of[(0, r)] = open_bank()
                     multiply(banks_of[(0, r)][:], r, c, *codes)
 
-        w_grouped = regroup_w_chunk(0, 0, VECTOR_EIGHTHS_FIRST)
-        quantise_w_chunk(0, 0, w_grouped, *codes)
         x_grouped_0 = collect_and_transpose_ahead(0)
-        w_grouped = regroup_w_chunk(0, 1, VECTOR_EIGHTHS_FIRST)
-        x_grouped_1 = collect_and_transpose_ahead(1)
+        w_grouped = regroup_w_chunk(0, 0, VECTOR_EIGHTHS_FIRST)
         quantise_x_block(0, x_grouped_0)
-        quantise_w_chunk(0, 1, w_grouped, *codes)
-        quantise_x_block(1, x_grouped_1)
-        multiply_first_group((0, 1), (0, 1))
+        quantise_w_chunk(0, 0, w_grouped, *codes)
+        x_grouped_1 = collect_and_transpose_ahead(1)
         x_grouped_2 = collect_and_transpose_ahead(2)
-        x_grouped_3 = collect_and_transpose_ahead(3)
+        quantise_x_block(1, x_grouped_1)
         quantise_x_block(2, x_grouped_2)
+        multiply_first_group((0, 1, 2), (0,))
+        w_grouped = regroup_w_chunk(0, 1, VECTOR_EIGHTHS_FIRST)
+        x_grouped_3 = collect_and_transpose_ahead(3)
+        quantise_w_chunk(0, 1, w_grouped, *codes)
         quantise_x_block(3, x_grouped_3)
-        multiply_first_group((2, 3), (0, 1))
+        multiply_first_group((0, 1, 2), (1,))
+        multiply_first_group((3,), (0, 1))
         for c in range(2, PASSES):
             w_grouped = regroup_w_chunk(0, c, VECTOR_EIGHTHS_FIRST)
             quantise_w_chunk(0, c, w_grouped, *codes)
             multiply_first_group(range(TOKEN_BLOCKS), (c,))
 
-        w_grouped_next = regroup_w_chunk(1, 0, VECTOR_EIGHTHS_LATER)
+        interleaved_of = {PASSES + 1: interleave_on_tensor(1, 1)}
+        w_grouped_next = regroup_w_chunk(1, 0, VECTOR_EIGHTHS_FIRST)
         steps = len(widths) * PASSES
         for n in range(PASSES, steps):
             g, c = divmod(n, PASSES)
@@ -272,6 +313,9 @@ def tile_multiqueryattention_pa_kernel(tc, x, sin, cos, W_qkv, out_0, out_1, out
                     [P, GROUP_HEADS, TOKEN_BLOCKS, HEAD_DIM], F32, tag="rotated"
                 )
                 codes = open_codes()
+            ahead = n + TENSOR_AHEAD
+            if ahead < steps:
+                interleaved_of[ahead] = interleave_on_tensor(ahead // PASSES, ahead % PASSES)
             if g > 1 and c + 1 < TOKEN_BLOCKS:
                 banks_of[(g - 1, c + 1)] = multiply_bank(c + 1, *done_codes)
             if g == 1:
@@ -280,10 +324,8 @@ def tile_multiqueryattention_pa_kernel(tc, x, sin, cos, W_qkv, out_0, out_1, out
             if c == PASSES - 1 and g < Q_GROUPS:
                 banks_of[(g, 0)] = multiply_bank(0, *codes)
             if n + 1 < steps:
-                g_next, c_next = divmod(n + 1, PASSES)
-                helps = c_next == 0 and g_next <= VECTOR_HELPS_UNTIL
-                w_grouped_next = regroup_w_chunk(
-                    g_next, c_next, VECTOR_EIGHTHS_LATER if helps else 0
+                w_grouped_next = collect_w_chunk(
+                    (n + 1) // PASSES, (n + 1) % PASSES, interleaved_of[n + 1]
                 )
             if g > 1:
                 rope_q_bank(c, banks_of[(g - 1, c)], rotated)

@@ -88,9 +88,8 @@ def tile_multiqueryattention_pa_kernel(tc, x, sin, cos, W_qkv, out_0, out_1, out
             if c < X_PAIRS:
                 for r in range(2 * c + 1, min(2 * c + 3, TOKEN_BLOCKS)):
                     x_rows_of.append(load_x_block(r))
-            if c == X_PAIRS - 1:
-                nc.sync.dma_start(out=cos_raw[:], in_=cos_blocks)
-                nc.sync.dma_start(out=sin_raw[:], in_=sin_blocks)
+        nc.sync.dma_start(out=sin_raw[:], in_=sin_blocks)
+        nc.sync.dma_start(out=cos_raw[:], in_=cos_blocks)
         for g in range(1, len(widths)):
             for c in range(PASSES):
                 w_raw_of[(g, c)] = load_w_chunk(g, c)
@@ -105,20 +104,15 @@ def tile_multiqueryattention_pa_kernel(tc, x, sin, cos, W_qkv, out_0, out_1, out
         identity_bf16 = const.tile([P, P], BF16)
         make_identity(nc, identity_bf16[:])
 
-        def make_tables(factor):
-            tables = const.tile([P, 2, TOKEN_BLOCKS, HEAD_DIM], F32, name="tables_%d" % (factor == 1.0))
-            for out, in_, signed in (
-                (tables[:, 0], cos_raw[:], factor),
-                (tables[:, 1, :, 0:HALF], sin_raw[:, :, HALF:HEAD_DIM], factor),
-                (tables[:, 1, :, HALF:HEAD_DIM], sin_raw[:, :, 0:HALF], -factor),
-            ):
-                nc.gpsimd.tensor_scalar(
-                    out=out, in0=in_, scalar1=signed, scalar2=0.0, op0=MULT, op1=ADD
-                )
-            return tables
+        tables_q = const.tile([P, 2, TOKEN_BLOCKS, HEAD_DIM], F32)
+        tables_k = const.tile([P, 2, TOKEN_BLOCKS, HEAD_DIM], F32)
 
-        tables_q = make_tables(Q_SCALE)
-        tables_k = make_tables(1.0)
+        halves = ((slice(0, HALF), slice(HALF, HEAD_DIM), 1.0), (slice(HALF, HEAD_DIM), slice(0, HALF), -1.0))
+        for here, other, sign in halves:
+            nc.gpsimd.tensor_scalar(
+                out=tables_q[:, 1, :, here], in0=sin_raw[:, :, other],
+                scalar1=sign * Q_SCALE, scalar2=0.0, op0=MULT, op1=ADD,
+            )
 
         warm_weights = const.tile([P, P], BF16)
         warm_moving = const.tile([P, GROUP_COLS], BF16)
@@ -246,7 +240,7 @@ def tile_multiqueryattention_pa_kernel(tc, x, sin, cos, W_qkv, out_0, out_1, out
         def swap_halves(u):
             return u.rearrange("p h (s d) -> p h s d", s=2)[:, :, ::-1, :]
 
-        def rope_q_bank(r, bank, rotated):
+        def rope_q_bank(r, bank, rotated, adder):
             products = product_pool.tile([P, 2, GROUP_HEADS, HEAD_DIM], F32)
             shape = [P, 2, GROUP_HEADS, HEAD_DIM]
             heads = bank[:].rearrange("p (h d) -> p h d", d=HEAD_DIM)
@@ -256,7 +250,7 @@ def tile_multiqueryattention_pa_kernel(tc, x, sin, cos, W_qkv, out_0, out_1, out
                 in1=tables_q[:, :, r, :].unsqueeze(2).to_broadcast(shape),
                 op=MULT,
             )
-            nc.gpsimd.tensor_tensor(
+            adder.tensor_tensor(
                 out=rotated[:, :, r, :].rearrange("p h (s d) -> p h s d", s=2),
                 in0=products[:, 0].rearrange("p h (s d) -> p h s d", s=2),
                 in1=swap_halves(products[:, 1]),
@@ -301,9 +295,12 @@ def tile_multiqueryattention_pa_kernel(tc, x, sin, cos, W_qkv, out_0, out_1, out
             quantise_w_chunk(0, c, w_grouped, *codes)
             multiply_first_group(range(TOKEN_BLOCKS), (c,))
 
+        nc.scalar.mul(tables_q[:, 0], cos_raw[:], Q_SCALE)
+
         interleaved_of = {PASSES + 1: interleave_on_tensor(1, 1)}
         w_grouped_next = regroup_w_chunk(1, 0, VECTOR_EIGHTHS_FIRST)
         steps = len(widths) * PASSES
+        kv_banks = []
         for n in range(PASSES, steps):
             g, c = divmod(n, PASSES)
             w_grouped = w_grouped_next
@@ -319,8 +316,18 @@ def tile_multiqueryattention_pa_kernel(tc, x, sin, cos, W_qkv, out_0, out_1, out
             if g > 1 and c + 1 < TOKEN_BLOCKS:
                 banks_of[(g - 1, c + 1)] = multiply_bank(c + 1, *done_codes)
             if g == 1:
-                rope_q_bank(c, banks_of[(g - 1, c)], rotated)
+                rope_q_bank(c, banks_of[(g - 1, c)], rotated, nc.gpsimd)
+            if n == steps - 1:
+                for r in range(TOKEN_BLOCKS):
+                    bank = psum_x.tile([P, GROUP_COLS], F32, tag="x_bank", name="kv_bank")
+                    kv_banks.append(bank[:, 0:KV_COLS])
+                for chunk in range(PASSES - 1):
+                    for r in range(TOKEN_BLOCKS):
+                        multiply(kv_banks[r], r, chunk, *codes)
             quantise_w_chunk(g, c, w_grouped, *codes)
+            if n == steps - 1:
+                for r in range(TOKEN_BLOCKS):
+                    multiply(kv_banks[r], r, PASSES - 1, *codes)
             if c == PASSES - 1 and g < Q_GROUPS:
                 banks_of[(g, 0)] = multiply_bank(0, *codes)
             if n + 1 < steps:
@@ -328,7 +335,8 @@ def tile_multiqueryattention_pa_kernel(tc, x, sin, cos, W_qkv, out_0, out_1, out
                     (n + 1) // PASSES, (n + 1) % PASSES, interleaved_of[n + 1]
                 )
             if g > 1:
-                rope_q_bank(c, banks_of[(g - 1, c)], rotated)
+                adder = nc.vector if n == steps - 1 else nc.gpsimd
+                rope_q_bank(c, banks_of[(g - 1, c)], rotated, adder)
             stored = TOKEN_BLOCKS if g < Q_GROUPS else TOKEN_BLOCKS // 2
             if (c + 1) % stored == 0:
                 heads = slice((g - 1) * GROUP_HEADS, g * GROUP_HEADS)
@@ -337,34 +345,27 @@ def tile_multiqueryattention_pa_kernel(tc, x, sin, cos, W_qkv, out_0, out_1, out
                     out=q_view[:, heads, blocks, :], in_=rotated[:, :, blocks, :]
                 )
 
+        nc.scalar.copy(out=tables_k[:, 0], in_=cos_raw[:])
+        for here, other, sign in halves:
+            nc.scalar.mul(tables_k[:, 1, :, here], sin_raw[:, :, other], sign)
+
         k_rows = out_pool.tile([P, TOKEN_BLOCKS, HEAD_DIM], F32, tag="k_rows")
         v_rows = out_pool.tile([P, TOKEN_BLOCKS, HEAD_DIM], F32, tag="v_rows")
-        kv_banks = []
-        for pair in range(2):
-            bank = psum_acc.tile([P, 2, KV_COLS], F32, tag="bank", name="acc")
-            for rr in range(2):
-                for c in range(PASSES):
-                    multiply(bank[:, rr, :], 2 * pair + rr, c, *codes)
-            kv_banks.append(bank)
-        products_of = []
-        for pair in range(2):
-            blocks = slice(2 * pair, 2 * pair + 2)
-            products = product_pool.tile([P, 2, 2, HEAD_DIM], F32)
+        products = product_pool.tile([P, 2, TOKEN_BLOCKS, HEAD_DIM], F32)
+        for r in range(TOKEN_BLOCKS):
+            bank = kv_banks[r]
             nc.vector.tensor_tensor(
-                out=products[:],
-                in0=kv_banks[pair][:, :, 0:HEAD_DIM].unsqueeze(1).to_broadcast([P, 2, 2, HEAD_DIM]),
-                in1=tables_k[:, :, blocks, :],
+                out=products[:, :, r, :],
+                in0=bank[:, 0:HEAD_DIM].unsqueeze(1).to_broadcast([P, 2, HEAD_DIM]),
+                in1=tables_k[:, :, r, :],
                 op=MULT,
             )
-            products_of.append(products)
-            nc.scalar.copy(out=v_rows[:, blocks, :], in_=kv_banks[pair][:, :, HEAD_DIM:KV_COLS])
-        for pair in range(2):
-            blocks = slice(2 * pair, 2 * pair + 2)
-            nc.vector.tensor_tensor(
-                out=k_rows[:, blocks, :].rearrange("p h (s d) -> p h s d", s=2),
-                in0=products_of[pair][:, 0].rearrange("p h (s d) -> p h s d", s=2),
-                in1=swap_halves(products_of[pair][:, 1]),
-                op=ADD,
-            )
-        nc.sync.dma_start(out=v_view, in_=v_rows[:].rearrange("p r d -> p (r d)"))
+            nc.scalar.copy(out=v_rows[:, r, :], in_=bank[:, HEAD_DIM:KV_COLS])
+        nc.vector.tensor_tensor(
+            out=k_rows[:].rearrange("p h (s d) -> p h s d", s=2),
+            in0=products[:, 0].rearrange("p h (s d) -> p h s d", s=2),
+            in1=swap_halves(products[:, 1]),
+            op=ADD,
+        )
         nc.sync.dma_start(out=k_view, in_=k_rows[:].rearrange("p r d -> p (r d)"))
+        nc.sync.dma_start(out=v_view, in_=v_rows[:].rearrange("p r d -> p (r d)"))

@@ -29,7 +29,7 @@ Q_GROUPS = Q_HEADS // GROUP_HEADS
 KV_COLS = 2 * HEAD_DIM
 Q_SCALE = HEAD_DIM**-0.5
 RUN = 4
-VECTOR_EIGHTHS_FIRST = 4
+VECTOR_EIGHTHS_FIRST = 5
 TENSOR_AHEAD = 2
 
 WARM_UP = 4
@@ -133,7 +133,8 @@ def tile_multiqueryattention_pa_kernel(tc, x, sin, cos, W_qkv, out_0, out_1, out
             x_banks = []
             for j in range(PASSES // 2):
                 bank = psum_x.tile([P, GROUP_COLS], F32, tag="x_bank")
-                keep_tensor_busy(bank, WARM_UP if r == 0 and j == 0 else 1)
+                if r == 0 and j == 0:
+                    keep_tensor_busy(bank, WARM_UP)
                 for cc in range(2):
                     for u in range(2):
                         word = 2 * P * (2 * j + cc)
@@ -149,12 +150,11 @@ def tile_multiqueryattention_pa_kernel(tc, x, sin, cos, W_qkv, out_0, out_1, out
             x_grouped = x_stage.tile([P, PASSES, P, PACK], BF16, align_bytes=64)
             words = x_grouped[:].rearrange("p c n t -> p (c n t)").bitcast(F32)
             words = words.rearrange("p (c n u) -> p c n u", c=PASSES, u=2)
-            nc.scalar.copy(
-                out=words[:, 0:2], in_=x_banks[0][:].rearrange("p (c u n) -> p c n u", c=2, u=2)
-            )
-            nc.vector.tensor_copy(
-                out=words[:, 2:4], in_=x_banks[1][:].rearrange("p (c u n) -> p c n u", c=2, u=2)
-            )
+            for j, bank in enumerate(x_banks):
+                nc.scalar.copy(
+                    out=words[:, 2 * j : 2 * j + 2],
+                    in_=bank[:].rearrange("p (c u n) -> p c n u", c=2, u=2),
+                )
             return x_grouped
 
         def quantise_x_block(r, x_grouped):
@@ -298,7 +298,7 @@ def tile_multiqueryattention_pa_kernel(tc, x, sin, cos, W_qkv, out_0, out_1, out
         nc.scalar.mul(tables_q[:, 0], cos_raw[:], Q_SCALE)
 
         interleaved_of = {PASSES + 1: interleave_on_tensor(1, 1)}
-        w_grouped_next = regroup_w_chunk(1, 0, VECTOR_EIGHTHS_FIRST)
+        w_grouped_next = regroup_w_chunk(1, 0, 0)
         steps = len(widths) * PASSES
         kv_banks = []
         for n in range(PASSES, steps):

from contextlib import ExitStack

import concourse.mybir as mybir
from concourse.masks import make_identity

F32 = mybir.dt.float32
BF16 = mybir.dt.bfloat16
U32 = mybir.dt.uint32
U8 = mybir.dt.uint8
FP8X4 = mybir.dt.float8_e4m3fn_x4
MULT = mybir.AluOpType.mult
ADD = mybir.AluOpType.add

P = 128
PACK = 4
K_PASS = P * PACK
TOKENS = 512
D_MODEL = 2048
HEAD_DIM = 128
HALF = HEAD_DIM // 2
Q_HEADS = 16
N_COLS = (Q_HEADS + 2) * HEAD_DIM
PASSES = D_MODEL // K_PASS
TOKEN_BLOCKS = TOKENS // P
X_PAIRS = TOKEN_BLOCKS // 2
GROUP_COLS = 512
GROUP_HEADS = GROUP_COLS // HEAD_DIM
Q_GROUPS = Q_HEADS // GROUP_HEADS
KV_COLS = 2 * HEAD_DIM
Q_SCALE = HEAD_DIM**-0.5
RUN = 4
VECTOR_EIGHTHS_FIRST = 5
TENSOR_AHEAD = 2

WARM_UP = 4

FLOPS = 2 * TOKENS * D_MODEL * N_COLS


def tile_multiqueryattention_pa_kernel(tc, x, sin, cos, W_qkv, out_0, out_1, out_2):
    nc = tc.nc
    widths = [GROUP_COLS] * Q_GROUPS + [KV_COLS]

    x_blocks = x.rearrange("b (m r) k -> (b m) r k", r=TOKEN_BLOCKS)
    cos_blocks = cos.rearrange("(m r) d -> m r d", r=TOKEN_BLOCKS)
    sin_blocks = sin.rearrange("(m r) d -> m r d", r=TOKEN_BLOCKS)
    q_view = out_0.rearrange("b h (m r) d -> m (b h) r d", r=TOKEN_BLOCKS)
    k_view = out_1.rearrange("b (m r) d -> (b m) (r d)", r=TOKEN_BLOCKS)
    v_view = out_2.rearrange("b (m r) d -> (b m) (r d)", r=TOKEN_BLOCKS)

    with ExitStack() as ctx:
        const = ctx.enter_context(tc.tile_pool(name="const", bufs=1))
        x_pool = ctx.enter_context(tc.tile_pool(name="x_pool", bufs=TOKEN_BLOCKS))
        x_stage = ctx.enter_context(tc.tile_pool(name="x_stage", bufs=TOKEN_BLOCKS))
        raw_pool = ctx.enter_context(tc.tile_pool(name="raw_pool", bufs=len(widths) * PASSES))
        grouped_pool = ctx.enter_context(tc.tile_pool(name="grouped_pool", bufs=4))
        codes_pool = ctx.enter_context(tc.tile_pool(name="codes_pool", bufs=3))
        product_pool = ctx.enter_context(tc.tile_pool(name="product_pool", bufs=4))
        out_pool = ctx.enter_context(tc.tile_pool(name="out_pool", bufs=3))
        psum_acc = ctx.enter_context(tc.psum_pool(name="psum_acc", bufs=TOKEN_BLOCKS))
        psum_x = ctx.enter_context(tc.psum_pool(name="psum_x", bufs=4))
        ctx.enter_context(tc.manual_schedule())

        def load_x_block(r):
            x_rows = x_pool.tile([P, D_MODEL], BF16)
            nc.sync.dma_start(out=x_rows[:], in_=x_blocks[:, r, :])
            return x_rows

        def load_w_chunk(g, c):
            first = g * GROUP_COLS
            w_raw = raw_pool.tile([P, PACK, widths[g]], BF16)
            w_rows = W_qkv[K_PASS * c : K_PASS * (c + 1), first : first + widths[g]].rearrange(
                "(p t) w -> p t w", t=PACK
            )
            for u in range(2):
                nc.sync.dma_start(
                    out=w_raw[:, 2 * u : 2 * u + 2, :], in_=w_rows[:, 2 * u : 2 * u + 2, :]
                )
            return w_raw

        cos_raw = const.tile([P, TOKEN_BLOCKS, HEAD_DIM], BF16)
        sin_raw = const.tile([P, TOKEN_BLOCKS, HEAD_DIM], BF16)

        x_rows_of = [load_x_block(0)]
        w_raw_of = {}
        for c in range(PASSES):
            w_raw_of[(0, c)] = load_w_chunk(0, c)
            if c < X_PAIRS:
                for r in range(2 * c + 1, min(2 * c + 3, TOKEN_BLOCKS)):
                    x_rows_of.append(load_x_block(r))
        nc.sync.dma_start(out=sin_raw[:], in_=sin_blocks)
        nc.sync.dma_start(out=cos_raw[:], in_=cos_blocks)
        for g in range(1, len(widths)):
            for c in range(PASSES):
                w_raw_of[(g, c)] = load_w_chunk(g, c)

        table_in = const.tile([P, 1], F32)
        table_out = const.tile([P, 1], F32)
        nc.gpsimd.memset(table_in[:], 0.0)
        nc.scalar.copy(out=table_out[:], in_=table_in[:])

        identity = const.tile([P, P], F32)
        make_identity(nc, identity[:])
        identity_bf16 = const.tile([P, P], BF16)
        make_identity(nc, identity_bf16[:])

        tables_q = const.tile([P, 2, TOKEN_BLOCKS, HEAD_DIM], F32)
        tables_k = const.tile([P, 2, TOKEN_BLOCKS, HEAD_DIM], F32)

        halves = ((slice(0, HALF), slice(HALF, HEAD_DIM), 1.0), (slice(HALF, HEAD_DIM), slice(0, HALF), -1.0))
        for here, other, sign in halves:
            nc.gpsimd.tensor_scalar(
                out=tables_q[:, 1, :, here], in0=sin_raw[:, :, other],
                scalar1=sign * Q_SCALE, scalar2=0.0, op0=MULT, op1=ADD,
            )

        warm_weights = const.tile([P, P], BF16)
        warm_moving = const.tile([P, GROUP_COLS], BF16)
        nc.vector.memset(warm_weights[:], 0.0)
        nc.vector.memset(warm_moving[:], 0.0)

        def keep_tensor_busy(bank, count):
            for i in range(count):
                nc.tensor.matmul(
                    bank[:], lhsT=warm_weights[:], rhs=warm_moving[:], start=True, stop=True
                )

        x_codes = const.tile([P, TOKEN_BLOCKS, PASSES, P], U32, align_bytes=64)
        x_scales = const.tile([P, TOKEN_BLOCKS, PASSES, P], U8, align_bytes=64)

        def transpose_x_block(r):
            x_words = x_rows_of[r][:].bitcast(F32)
            x_banks = []
            for j in range(PASSES // 2):
                bank = psum_x.tile([P, GROUP_COLS], F32, tag="x_bank")
                if r == 0 and j == 0:
                    keep_tensor_busy(bank, WARM_UP)
                for cc in range(2):
                    for u in range(2):
                        word = 2 * P * (2 * j + cc)
                        nc.tensor.transpose(
                            bank[:, (2 * cc + u) * P : (2 * cc + u + 1) * P],
                            x_words[:, word + u : word + 2 * P : 2],
                            identity[:],
                        )
                x_banks.append(bank)
            return x_banks

        def collect_x_block(x_banks):
            x_grouped = x_stage.tile([P, PASSES, P, PACK], BF16, align_bytes=64)
            words = x_grouped[:].rearrange("p c n t -> p (c n t)").bitcast(F32)
            words = words.rearrange("p (c n u) -> p c n u", c=PASSES, u=2)
            for j, bank in enumerate(x_banks):
                nc.scalar.copy(
                    out=words[:, 2 * j : 2 * j + 2],
                    in_=bank[:].rearrange("p (c u n) -> p c n u", c=2, u=2),
                )
            return x_grouped

        def quantise_x_block(r, x_grouped):
            nc.vector.quantize_mx(
                out=x_codes[:, r].rearrange("p c m -> p (c m)").bitcast(FP8X4),
                scales=x_scales[:, r].rearrange("p c m -> p (c m)"),
                in_=x_grouped[:].rearrange("p c n t -> p (c n t)"),
            )

        def regroup_w_chunk(g, c, vector_eighths):
            width = widths[g]
            split = width - width * vector_eighths // 8
            w_grouped = grouped_pool.tile([P, width, PACK], BF16, align_bytes=64)
            w_raw = w_raw_of[(g, c)]
            nc.scalar.copy(
                out=w_grouped[:, 0:split, :].rearrange("p (n i) t -> p n t i", i=RUN),
                in_=w_raw[:, :, 0:split].rearrange("p t (n i) -> p n t i", i=RUN),
            )
            if split < width:
                nc.vector.tensor_copy(
                    out=w_grouped[:, split:width, :].rearrange("p (n i) t -> p n t i", i=RUN),
                    in_=w_raw[:, :, split:width].rearrange("p t (n i) -> p n t i", i=RUN),
                )
            return w_grouped

        def interleave_on_tensor(g, c):
            bank = psum_x.tile([P, GROUP_COLS], F32, tag="x_bank", name="w_bank")
            words = bank[:].bitcast(BF16)[:, 0 : P * PACK]
            nc.tensor.matmul(
                words.rearrange("p (n t) -> p n t", t=PACK),
                lhsT=identity_bf16[:],
                rhs=w_raw_of[(g, c)][:, :, widths[g] - P : widths[g]].rearrange("p t n -> p n t"),
                start=True,
                stop=True,
            )
            return words

        def collect_w_chunk(g, c, interleaved):
            split = widths[g] - P
            w_grouped = grouped_pool.tile([P, widths[g], PACK], BF16, align_bytes=64, name="w_grouped")
            nc.scalar.copy(
                out=w_grouped[:, 0:split, :].rearrange("p (n i) t -> p n t i", i=RUN),
                in_=w_raw_of[(g, c)][:, :, 0:split].rearrange("p t (n i) -> p n t i", i=RUN),
            )
            nc.scalar.copy(
                out=w_grouped[:, split:, :].rearrange("p n t -> p (n t)"), in_=interleaved
            )
            return w_grouped

        def quantise_w_chunk(g, c, w_grouped, w_codes, w_scales):
            nc.vector.quantize_mx(
                out=w_codes[:, c, 0 : widths[g]].bitcast(FP8X4),
                scales=w_scales[:, c, 0 : widths[g]],
                in_=w_grouped[:].rearrange("p n t -> p (n t)"),
            )

        def open_codes():
            w_codes = codes_pool.tile([P, PASSES, GROUP_COLS], U32, align_bytes=64)
            w_scales = codes_pool.tile([P, PASSES, GROUP_COLS], U8, align_bytes=64)
            return w_codes, w_scales

        def multiply(out, r, c, w_codes, w_scales):
            width = out.shape[1]
            nc.tensor.matmul_mx(
                out=out,
                lhsT=x_codes[:, r, c, :].bitcast(FP8X4),
                lhsT_scale=x_scales[:, r, c, :],
                rhs=w_codes[:, c, 0:width].bitcast(FP8X4),
                rhs_scale=w_scales[:, c, 0:width],
                start=(c == 0),
                stop=(c == PASSES - 1),
            )

        def open_bank():
            return psum_acc.tile([P, GROUP_COLS], F32, tag="bank", name="acc")

        def multiply_bank(r, w_codes, w_scales):
            bank = open_bank()
            for c in range(PASSES):
                multiply(bank[:], r, c, w_codes, w_scales)
            return bank

        def swap_halves(u):
            return u.rearrange("p h (s d) -> p h s d", s=2)[:, :, ::-1, :]

        def rope_q_bank(r, bank, rotated, adder):
            products = product_pool.tile([P, 2, GROUP_HEADS, HEAD_DIM], F32)
            shape = [P, 2, GROUP_HEADS, HEAD_DIM]
            heads = bank[:].rearrange("p (h d) -> p h d", d=HEAD_DIM)
            nc.vector.tensor_tensor(
                out=products[:],
                in0=heads.unsqueeze(1).to_broadcast(shape),
                in1=tables_q[:, :, r, :].unsqueeze(2).to_broadcast(shape),
                op=MULT,
            )
            adder.tensor_tensor(
                out=rotated[:, :, r, :].rearrange("p h (s d) -> p h s d", s=2),
                in0=products[:, 0].rearrange("p h (s d) -> p h s d", s=2),
                in1=swap_halves(products[:, 1]),
                op=ADD,
            )

        assert PASSES == TOKEN_BLOCKS
        banks_of = {}
        codes = open_codes()
        x_banks_of = [transpose_x_block(r) for r in range(2)]

        def collect_and_transpose_ahead(r):
            x_grouped = collect_x_block(x_banks_of[r])
            if r + 2 < TOKEN_BLOCKS:
                x_banks_of.append(transpose_x_block(r + 2))
            return x_grouped

        def multiply_first_group(blocks, chunks):
            for c in chunks:
                for r in blocks:
                    if c == 0:
                        banks_of[(0, r)] = open_bank()
                    multiply(banks_of[(0, r)][:], r, c, *codes)

        x_grouped_0 = collect_and_transpose_ahead(0)
        w_grouped = regroup_w_chunk(0, 0, VECTOR_EIGHTHS_FIRST)
        quantise_x_block(0, x_grouped_0)
        quantise_w_chunk(0, 0, w_grouped, *codes)
        x_grouped_1 = collect_and_transpose_ahead(1)
        x_grouped_2 = collect_and_transpose_ahead(2)
        quantise_x_block(1, x_grouped_1)
        quantise_x_block(2, x_grouped_2)
        multiply_first_group((0, 1, 2), (0,))
        w_grouped = regroup_w_chunk(0, 1, VECTOR_EIGHTHS_FIRST)
        x_grouped_3 = collect_and_transpose_ahead(3)
        quantise_w_chunk(0, 1, w_grouped, *codes)
        quantise_x_block(3, x_grouped_3)
        multiply_first_group((0, 1, 2), (1,))
        multiply_first_group((3,), (0, 1))
        for c in range(2, PASSES):
            w_grouped = regroup_w_chunk(0, c, VECTOR_EIGHTHS_FIRST)
            quantise_w_chunk(0, c, w_grouped, *codes)
            multiply_first_group(range(TOKEN_BLOCKS), (c,))

        nc.scalar.mul(tables_q[:, 0], cos_raw[:], Q_SCALE)

        interleaved_of = {PASSES + 1: interleave_on_tensor(1, 1)}
        w_grouped_next = regroup_w_chunk(1, 0, 0)
        steps = len(widths) * PASSES
        kv_banks = []
        for n in range(PASSES, steps):
            g, c = divmod(n, PASSES)
            w_grouped = w_grouped_next
            if c == 0:
                done_codes = codes
                rotated = out_pool.tile(
                    [P, GROUP_HEADS, TOKEN_BLOCKS, HEAD_DIM], F32, tag="rotated"
                )
                codes = open_codes()
            ahead = n + TENSOR_AHEAD
            if ahead < steps:
                interleaved_of[ahead] = interleave_on_tensor(ahead // PASSES, ahead % PASSES)
            if g > 1 and c + 1 < TOKEN_BLOCKS:
                banks_of[(g - 1, c + 1)] = multiply_bank(c + 1, *done_codes)
            if g == 1:
                rope_q_bank(c, banks_of[(g - 1, c)], rotated, nc.gpsimd)
            if n == steps - 1:
                for r in range(TOKEN_BLOCKS):
                    bank = psum_x.tile([P, GROUP_COLS], F32, tag="x_bank", name="kv_bank")
                    kv_banks.append(bank[:, 0:KV_COLS])
                for chunk in range(PASSES - 1):
                    for r in range(TOKEN_BLOCKS):
                        multiply(kv_banks[r], r, chunk, *codes)
            quantise_w_chunk(g, c, w_grouped, *codes)
            if n == steps - 1:
                for r in range(TOKEN_BLOCKS):
                    multiply(kv_banks[r], r, PASSES - 1, *codes)
            if c == PASSES - 1 and g < Q_GROUPS:
                banks_of[(g, 0)] = multiply_bank(0, *codes)
            if n + 1 < steps:
                w_grouped_next = collect_w_chunk(
                    (n + 1) // PASSES, (n + 1) % PASSES, interleaved_of[n + 1]
                )
            if g > 1:
                adder = nc.vector if n == steps - 1 else nc.gpsimd
                rope_q_bank(c, banks_of[(g - 1, c)], rotated, adder)
            stored = TOKEN_BLOCKS if g < Q_GROUPS else TOKEN_BLOCKS // 2
            if (c + 1) % stored == 0:
                heads = slice((g - 1) * GROUP_HEADS, g * GROUP_HEADS)
                blocks = slice(c + 1 - stored, c + 1)
                nc.sync.dma_start(
                    out=q_view[:, heads, blocks, :], in_=rotated[:, :, blocks, :]
                )

        nc.scalar.copy(out=tables_k[:, 0], in_=cos_raw[:])
        for here, other, sign in halves:
            nc.scalar.mul(tables_k[:, 1, :, here], sin_raw[:, :, other], sign)

        k_rows = out_pool.tile([P, TOKEN_BLOCKS, HEAD_DIM], F32, tag="k_rows")
        v_rows = out_pool.tile([P, TOKEN_BLOCKS, HEAD_DIM], F32, tag="v_rows")
        products = product_pool.tile([P, 2, TOKEN_BLOCKS, HEAD_DIM], F32)
        for r in range(TOKEN_BLOCKS):
            bank = kv_banks[r]
            nc.vector.tensor_tensor(
                out=products[:, :, r, :],
                in0=bank[:, 0:HEAD_DIM].unsqueeze(1).to_broadcast([P, 2, HEAD_DIM]),
                in1=tables_k[:, :, r, :],
                op=MULT,
            )
            nc.scalar.copy(out=v_rows[:, r, :], in_=bank[:, HEAD_DIM:KV_COLS])
        nc.vector.tensor_tensor(
            out=k_rows[:].rearrange("p h (s d) -> p h s d", s=2),
            in0=products[:, 0].rearrange("p h (s d) -> p h s d", s=2),
            in1=swap_halves(products[:, 1]),
            op=ADD,
        )
        nc.sync.dma_start(out=k_view, in_=k_rows[:].rearrange("p r d -> p (r d)"))
        nc.sync.dma_start(out=v_view, in_=v_rows[:].rearrange("p r d -> p (r d)"))
